import numpy as np
import ml_dtypes


def mxq(x, axis, fmt="e4m3"):
    dtype, down = {"e4m3": (ml_dtypes.float8_e4m3fn, 7), "e5m2": (ml_dtypes.float8_e5m2, 14)}[fmt]
    v = np.moveaxis(np.asarray(x, np.float32).astype(ml_dtypes.bfloat16).astype(np.float64), axis, -1)
    blocks = v.reshape(v.shape[:-1] + (-1, 32))
    amax = np.abs(blocks).max(-1, keepdims=True)
    byte = np.maximum(np.where(amax > 0, np.frexp(amax)[1] - 1 + 127, 0) - down, 1)
    scale = np.exp2(byte - 127.0)
    codes = (blocks / scale).astype(np.float32).astype(dtype).astype(np.float64)
    return np.moveaxis((codes * scale).reshape(v.shape), -1, axis)


WIDE = False


def mx_kscale(k):
    if not WIDE:
        return np.ones(k)
    levels = np.array([10, -10, 5, -5, 0])
    a = np.random.permutation(np.resize(levels, k // 512 * 4)).reshape(k // 512, 4)
    idx = np.arange(k)
    return np.exp2(a[idx // 512, idx % 128 // 32])


BF16 = ml_dtypes.bfloat16


def bf(x):
    return np.asarray(x, np.float32).astype(BF16)


def f64(x):
    return np.asarray(x).astype(np.float64)


E2M1 = np.array([0.0, 0.5, 1.0, 1.5, 2.0, 3.0, 4.0, 6.0, -0.0, -0.5, -1.0, -1.5, -2.0, -3.0, -4.0, -6.0])


def pack_weight(w, fmt):
    k, n = w.shape
    w = f64(bf(w)).reshape(k // 32, 32, n)
    amax = np.abs(w).max(1)
    if fmt == "e4m3":
        byte = np.frexp(amax)[1] - 1 + 127 - 7
    else:
        mant, ex = np.frexp(amax / 6.0)
        byte = np.where(mant > 0.5, ex, ex - 1) + 127
    byte = np.clip(np.where(amax > 0, byte, 1), 1, 254)
    scaled = (w * np.exp2(127.0 - byte)[:, None, :]).reshape(k, n).astype(np.float32)
    by_word = np.ascontiguousarray(scaled.reshape(k // 512, 128, 4, n).transpose(0, 1, 3, 2))
    if fmt == "e4m3":
        words = by_word.astype(ml_dtypes.float8_e4m3fn).view(np.uint8)
    else:
        c = by_word.astype(ml_dtypes.float4_e2m1fn).view(np.uint8) & 0xF
        words = c[..., 0::2] | (c[..., 1::2] << 4)
    return np.ascontiguousarray(words), np.ascontiguousarray(byte.astype(np.uint8).reshape(k // 512, 16, n))


def unpack_weight(words, scales, fmt):
    g, p, n, _ = words.shape
    if fmt == "e4m3":
        vals = np.ascontiguousarray(words).view(ml_dtypes.float8_e4m3fn).astype(np.float64)
    else:
        nib = np.empty((g, p, n, 4), np.uint8)
        nib[..., 0::2] = words & 0xF
        nib[..., 1::2] = words >> 4
        vals = E2M1[nib]
    vals = vals * np.repeat(np.exp2(scales.astype(np.float64) - 127.0), 8, axis=1)[..., None]
    return vals.transpose(0, 1, 3, 2).reshape(g * 512, n)

def pack4(w):
    words, scales = pack_weight(w, "e2m1")
    return words.reshape(words.shape[0], 128, -1), scales


def unpack4(words, scales):
    return unpack_weight(words.reshape(words.shape[0], 128, -1, 2), scales, "e2m1")


B, T, KA, KT, DIM, NH, HD, E = 16, 512, 256, 256, 512, 1, 128, 8
ROPE_BASE = 10000.0


def rope_cos_sin(L, hd):
    inv_freq = 1.0 / (ROPE_BASE ** (f64(np.arange(0, hd, 2)) / hd))
    freqs = f64(np.arange(L))[:, None] * inv_freq[None, :]
    emb = np.concatenate([freqs, freqs], axis=-1)
    return np.cos(emb), np.sin(emb)


def rotate_half(x):
    x1 = x[..., 0::2]
    x2 = x[..., 1::2]
    return np.stack((-x2, x1), axis=-1).reshape(x.shape)


def rope(t, cos, sin):
    return t * cos[None, None] + rotate_half(t) * sin[None, None]


def heads(t):
    return t.reshape(B, -1, NH, HD).transpose(0, 2, 1, 3)


def setup_inputs():
    s = mx_kscale(DIM)
    c = 1.2 / np.sqrt(DIM)
    x = bf(np.random.standard_normal((B, T, DIM)) * s)
    qa_words, qa_scales = pack4((np.random.standard_normal((NH * HD, DIM)) * c / s[None, :]).T)
    b_qa = bf(np.random.standard_normal(NH * HD) * 0.3)
    qt_words, qt_scales = pack4((np.random.standard_normal((NH * HD, DIM)) * c / s[None, :]).T)
    b_qt = bf(np.random.standard_normal(NH * HD) * 0.3)
    return {"x": x,
            "W_qa_words": qa_words,
            "W_qa_scales": qa_scales,
            "b_qa": b_qa,
            "W_qt_words": qt_words,
            "W_qt_scales": qt_scales,
            "b_qt": b_qt}


def reference(x, W_qa_words, W_qa_scales, b_qa, W_qt_words, W_qt_scales, b_qt):
    xq = mxq(f64(x), 2, "e4m3")
    q_a = heads((xq @ unpack4(W_qa_words, W_qa_scales)) + f64(b_qa))
    q_t = heads((xq @ unpack4(W_qt_words, W_qt_scales)) + f64(b_qt))
    cos_m, sin_m = rope_cos_sin(T, HD)
    return rope(q_a, cos_m, sin_m), rope(q_t, cos_m, sin_m)

@@ -1,0 +1,225 @@
+import math
+from contextlib import ExitStack
+
+import concourse.masks as masks
+import concourse.mybir as mybir
+
+F32 = mybir.dt.float32
+BF16 = mybir.dt.bfloat16
+I32 = mybir.dt.int32
+U32 = mybir.dt.uint32
+U8 = mybir.dt.uint8
+FP8X4 = mybir.dt.float8_e4m3fn_x4
+FP4X4 = mybir.dt.float4_e2m1fn_x4
+ALU = mybir.AluOpType
+ACT = mybir.ActivationFunctionType
+
+P = 128
+BATCH = 16
+T = 512
+K = 512
+D = 128
+SUB = T // P
+HALF = D // 2
+ROPE_BASE = 10000.0
+TWO_PI = 2.0 * math.pi
+ROUND = 1.5 * 2.0**23
+
+FLOPS = 2 * BATCH * T * K * 2 * D
+
+
+def tile_l1regressionmoeactionhead_pa_t_kernel(
+    tc, x, W_qa_words, W_qa_scales, b_qa, W_qt_words, W_qt_scales, b_qt, out_0, out_1
+):
+    nc = tc.nc
+    outs = (out_0, out_1)
+    weights = ((W_qa_words, W_qa_scales, b_qa), (W_qt_words, W_qt_scales, b_qt))
+
+    with ExitStack() as ctx:
+        keep = ctx.enter_context(tc.tile_pool(name="keep", bufs=1))
+        work = ctx.enter_context(tc.tile_pool(name="work", bufs=2))
+        psum = ctx.enter_context(tc.psum_pool(name="psum", bufs=2))
+        ctx.enter_context(tc.manual_schedule())
+
+        x_sb = keep.tile([P, BATCH, SUB, K], BF16)
+
+        def load_x(n):
+            nc.sync.dma_start(out=x_sb[:, n], in_=x[n].rearrange("(p c) k -> p c k", c=SUB))
+
+        load_x(0)
+
+        w_words = keep.tile([P, 2, 2 * D], U8, align_bytes=64)
+        w_scales = keep.tile([P, 2, D], U8, align_bytes=64)
+        bias_rows = keep.tile([P, P], BF16)
+        nc.vector.memset(w_scales[:].bitcast(I32), 0)
+        nc.vector.memset(bias_rows[:], 0.0)
+        for w, (words, scales, bias) in enumerate(weights):
+            nc.sync.dma_start(out=w_words[:, w, :].bitcast(I32), in_=words[0].bitcast(I32))
+            for q in range(4):
+                nc.sync.dma_start(
+                    out=w_scales[32 * q : 32 * q + 4, w, :].bitcast(I32),
+                    in_=scales[0, 4 * q : 4 * q + 4, :].bitcast(I32),
+                )
+            nc.scalar.dma_start(out=bias_rows[w : w + 1, :], in_=bias.unsqueeze(0))
+        for n in range(1, BATCH):
+            load_x(n)
+
+        warm = keep.tile([P, 1], F32)
+        nc.vector.memset(warm[:], 0.0)
+        nc.scalar.activation(out=warm[:], in_=warm[:], func=ACT.Sin)
+
+        ident = keep.tile([P, P], F32)
+        masks.make_identity(nc, ident[:])
+        position = keep.tile([P, SUB, P], F32)
+        nc.gpsimd.iota(
+            position[:],
+            pattern=[[1, SUB], [SUB, P]],
+            base=0,
+            channel_multiplier=0,
+            allow_small_or_imprecise_dtypes=True,
+        )
+
+        rows = keep.tile([P, 3, P], F32)
+        ratio = ROPE_BASE ** (-1.0 / HALF)
+        nc.vector.memset(rows[:, 0, 0:1], 1.0)
+        for doubling in range(6):
+            width = 2**doubling
+            nc.vector.tensor_scalar_mul(
+                out=rows[:, 0, width : 2 * width], in0=rows[:, 0, 0:width], scalar1=ratio**width
+            )
+        nc.vector.tensor_copy(out=rows[:, 0, HALF:D], in_=rows[:, 0, 0:HALF])
+        own = rows[:, 0, :].rearrange("p (i e) -> p i e", e=2)
+        partner = rows[:, 1, :].rearrange("p (i e) -> p i e", e=2)
+        nc.vector.tensor_copy(out=partner[:, :, 0], in_=own[:, :, 1])
+        nc.vector.tensor_scalar_mul(out=partner[:, :, 1], in0=own[:, :, 0], scalar1=-1.0)
+        nc.vector.tensor_copy(out=rows[:, 2, :], in_=bias_rows[:])
+
+        swap = keep.tile([P, P], F32)
+        ident_pairs = ident[:].rearrange("p (i e) -> p i e", e=2)
+        swap_pairs = swap[:].rearrange("p (i e) -> p i e", e=2)
+        nc.vector.tensor_copy(out=swap_pairs[:, :, 0], in_=ident_pairs[:, :, 1])
+        nc.vector.tensor_copy(out=swap_pairs[:, :, 1], in_=ident_pairs[:, :, 0])
+
+        columns = psum.tile([P, 3, P], F32, tag="rotated")
+        for r in range(3):
+            nc.tensor.transpose(columns[:, r, :], rows[:, r, :], ident[:])
+        per_feature = keep.tile([P, 4], F32)
+        nc.vector.tensor_scalar_mul(
+            out=per_feature[:, 0:2], in0=columns[:, 0:2, 0], scalar1=1.0 / TWO_PI
+        )
+        nc.vector.tensor_copy(out=per_feature[:, 2:4], in_=columns[:, 2, 0:2])
+
+        turns = keep.tile([P, 2, T], F32)
+        whole = keep.tile([P, 2, T], F32)
+        table = keep.tile([P, 2, T], F32)
+        for s, quarter in enumerate((0.25, 0.0)):
+            nc.vector.tensor_scalar(
+                out=turns[:, s, :],
+                in0=position[:].rearrange("p c t -> p (c t)"),
+                scalar1=per_feature[:, s : s + 1],
+                scalar2=quarter,
+                op0=ALU.mult,
+                op1=ALU.add,
+            )
+        nc.vector.tensor_scalar(
+            out=whole[:], in0=turns[:], scalar1=ROUND, scalar2=ROUND, op0=ALU.add, op1=ALU.subtract
+        )
+        nc.vector.tensor_sub(out=turns[:], in0=turns[:], in1=whole[:])
+
+        grouped_of = {}
+        codes_of = {}
+        acc_of = {}
+        products_of = {}
+
+        def transpose_x(n):
+            grouped = work.tile([P, T * 4], BF16, align_bytes=64, name="grouped")
+            grouped_words = grouped[:].bitcast(F32).rearrange("p (c t u) -> p c t u", c=SUB, u=2)
+            for h in range(SUB // 2):
+                xt = psum.tile([P, 2, 2, P], F32, name="xt")
+                for c in range(2):
+                    x_words = x_sb[:, n, 2 * h + c, :].bitcast(F32)
+                    for u in range(2):
+                        nc.tensor.transpose(xt[:, c, u, :], x_words[:, u : K // 2 : 2], ident[:])
+                nc.scalar.copy(
+                    out=grouped_words[:, 2 * h : 2 * h + 2],
+                    in_=xt[:].rearrange("p c u t -> p c t u"),
+                )
+            grouped_of[n] = grouped
+
+        def quantise(n):
+            codes = work.tile([P, T], U32, align_bytes=64, name="codes")
+            plane = work.tile([P, T], U8, align_bytes=64, name="plane")
+            nc.vector.quantize_mx(
+                out=codes[:].bitcast(FP8X4), scales=plane[:], in_=grouped_of[n][:]
+            )
+            codes_of[n] = (codes, plane)
+
+        def project(n):
+            codes, plane = codes_of[n]
+            for w in range(2):
+                acc = psum.tile([P, T], F32, name="acc", bufs=4)
+                nc.tensor.matmul_mx(
+                    out=acc[:],
+                    lhsT=w_words[:, w, :].bitcast(FP4X4),
+                    lhsT_scale=w_scales[:, w, :],
+                    rhs=codes[:].bitcast(FP8X4),
+                    rhs_scale=plane[:],
+                    start=True,
+                    stop=True,
+                )
+                acc_of[n, w] = acc
+
+        def multiply(n, w):
+            products = work.tile([P, 2, T], F32, name="products", bufs=4)
+            nc.vector.scalar_tensor_tensor(
+                out=products[:],
+                in0=acc_of[n, w][:].unsqueeze(1).to_broadcast([P, 2, T]),
+                scalar=per_feature[:, 2 + w : 3 + w],
+                in1=table[:],
+                op0=ALU.add,
+                op1=ALU.mult,
+            )
+            products_of[n, w] = products
+
+        def rotate_and_store(n):
+            for w in range(2):
+                products = products_of[n, w]
+                rotated = psum.tile([P, SUB, D], F32, name="rotated")
+                for c in range(SUB):
+                    tokens = slice(c * P, (c + 1) * P)
+                    nc.tensor.matmul(
+                        out=rotated[:, c, :],
+                        lhsT=products[:, 0, tokens],
+                        rhs=ident[:],
+                        is_transpose=True,
+                        start=True,
+                        stop=False,
+                    )
+                    nc.tensor.matmul(
+                        out=rotated[:, c, :],
+                        lhsT=products[:, 1, tokens],
+                        rhs=swap[:],
+                        is_transpose=True,
+                        start=False,
+                        stop=True,
+                    )
+                result = work.tile([P, SUB, D], F32, name="result", bufs=4)
+                nc.scalar.copy(out=result[:], in_=rotated[:])
+                nc.sync.dma_start(
+                    out=outs[w][n, 0].rearrange("(p c) d -> p c d", c=SUB), in_=result[:]
+                )
+
+        transpose_x(0)
+        quantise(0)
+        nc.scalar.activation(out=table[:], in_=turns[:], func=ACT.Sin, scale=TWO_PI)
+        for n in range(BATCH):
+            if n + 1 < BATCH:
+                transpose_x(n + 1)
+            project(n)
+            multiply(n, 0)
+            if n + 1 < BATCH:
+                quantise(n + 1)
+            multiply(n, 1)
+            if n >= 1:
+                rotate_and_store(n - 1)
+        rotate_and_store(BATCH - 1)

@@ -70,66 +70,68 @@ def tile_l1regressionmoeactionhead_pa_t_kernel(
 
         ident = keep.tile([P, P], F32)
         masks.make_identity(nc, ident[:])
-        position = keep.tile([P, SUB, P], F32)
+        position = keep.tile([P, SUB], F32)
         nc.gpsimd.iota(
             position[:],
-            pattern=[[1, SUB], [SUB, P]],
+            pattern=[[1, SUB]],
             base=0,
-            channel_multiplier=0,
+            channel_multiplier=SUB,
             allow_small_or_imprecise_dtypes=True,
         )
 
-        rows = keep.tile([P, 3, P], F32)
+        bias_rows_f32 = keep.tile([P, P], F32)
+        nc.vector.tensor_copy(out=bias_rows_f32[:], in_=bias_rows[:])
+        bias_columns = psum.tile([P, P], F32, tag="back", bufs=4)
+        nc.tensor.transpose(bias_columns[:], bias_rows_f32[:], ident[:])
+        bias_of = keep.tile([P, 2], F32)
+        nc.vector.tensor_copy(out=bias_of[:], in_=bias_columns[:, 0:2])
+
+        pace = keep.tile([P, HALF], F32)
         ratio = ROPE_BASE ** (-1.0 / HALF)
-        nc.vector.memset(rows[:, 0, 0:1], 1.0)
+        nc.vector.memset(pace[:, 0:1], 1.0)
         for doubling in range(6):
             width = 2**doubling
             nc.vector.tensor_scalar_mul(
-                out=rows[:, 0, width : 2 * width], in0=rows[:, 0, 0:width], scalar1=ratio**width
+                out=pace[:, width : 2 * width], in0=pace[:, 0:width], scalar1=ratio**width
             )
-        nc.vector.tensor_copy(out=rows[:, 0, HALF:D], in_=rows[:, 0, 0:HALF])
-        own = rows[:, 0, :].rearrange("p (i e) -> p i e", e=2)
-        partner = rows[:, 1, :].rearrange("p (i e) -> p i e", e=2)
-        nc.vector.tensor_copy(out=partner[:, :, 0], in_=own[:, :, 1])
-        nc.vector.tensor_scalar_mul(out=partner[:, :, 1], in0=own[:, :, 0], scalar1=-1.0)
-        nc.vector.tensor_copy(out=rows[:, 2, :], in_=bias_rows[:])
+        nc.vector.tensor_scalar_mul(out=pace[:], in0=pace[:], scalar1=1.0 / TWO_PI)
 
-        swap = keep.tile([P, P], F32)
-        ident_pairs = ident[:].rearrange("p (i e) -> p i e", e=2)
-        swap_pairs = swap[:].rearrange("p (i e) -> p i e", e=2)
-        nc.vector.tensor_copy(out=swap_pairs[:, :, 0], in_=ident_pairs[:, :, 1])
-        nc.vector.tensor_copy(out=swap_pairs[:, :, 1], in_=ident_pairs[:, :, 0])
-
-        columns = psum.tile([P, 3, P], F32, tag="rotated")
-        for r in range(3):
-            nc.tensor.transpose(columns[:, r, :], rows[:, r, :], ident[:])
-        per_feature = keep.tile([P, 4], F32)
-        nc.vector.tensor_scalar_mul(
-            out=per_feature[:, 0:2], in0=columns[:, 0:2, 0], scalar1=1.0 / TWO_PI
+        turns = keep.tile([P, 2, SUB, HALF], F32)
+        whole = keep.tile([P, 2, SUB, HALF], F32)
+        nc.vector.tensor_tensor(
+            out=turns[:, 1],
+            in0=position[:].unsqueeze(2).to_broadcast([P, SUB, HALF]),
+            in1=pace[:].unsqueeze(1).to_broadcast([P, SUB, HALF]),
+            op=ALU.mult,
         )
-        nc.vector.tensor_copy(out=per_feature[:, 2:4], in_=columns[:, 2, 0:2])
-
-        turns = keep.tile([P, 2, T], F32)
-        whole = keep.tile([P, 2, T], F32)
-        table = keep.tile([P, 2, T], F32)
-        for s, quarter in enumerate((0.25, 0.0)):
-            nc.vector.tensor_scalar(
-                out=turns[:, s, :],
-                in0=position[:].rearrange("p c t -> p (c t)"),
-                scalar1=per_feature[:, s : s + 1],
-                scalar2=quarter,
-                op0=ALU.mult,
-                op1=ALU.add,
-            )
+        nc.vector.tensor_scalar_add(out=turns[:, 0], in0=turns[:, 1], scalar1=0.25)
         nc.vector.tensor_scalar(
             out=whole[:], in0=turns[:], scalar1=ROUND, scalar2=ROUND, op0=ALU.add, op1=ALU.subtract
         )
         nc.vector.tensor_sub(out=turns[:], in0=turns[:], in1=whole[:])
 
+        table = keep.tile([P, 2, SUB, D], F32)
+
+        def fill_tables():
+            nc.scalar.activation(
+                out=table[:, 0].rearrange("p c (h j) -> p c h j", h=2),
+                in_=turns[:, 0].unsqueeze(2).to_broadcast([P, SUB, 2, HALF]),
+                func=ACT.Sin,
+                scale=TWO_PI,
+            )
+            to_partner = table[:, 1].rearrange("p c (h i e) -> p c h i e", h=2, e=2)
+            angle_pairs = turns[:, 1].rearrange("p c (i e) -> p c i e", e=2)
+            for e, sign in enumerate((1.0, -1.0)):
+                nc.scalar.activation(
+                    out=to_partner[:, :, :, :, e],
+                    in_=angle_pairs[:, :, :, 1 - e].unsqueeze(2).to_broadcast([P, SUB, 2, HALF // 2]),
+                    func=ACT.Sin,
+                    scale=sign * TWO_PI,
+                )
+
         grouped_of = {}
         codes_of = {}
-        acc_of = {}
-        products_of = {}
+        biased_of = {}
 
         def transpose_x(n):
             grouped = work.tile([P, T * 4], BF16, align_bytes=64, name="grouped")
@@ -157,7 +159,7 @@ def tile_l1regressionmoeactionhead_pa_t_kernel(
         def project(n):
             codes, plane = codes_of[n]
             for w in range(2):
-                acc = psum.tile([P, T], F32, name="acc", bufs=4)
+                acc = psum.tile([P, T], F32, name="acc")
                 nc.tensor.matmul_mx(
                     out=acc[:],
                     lhsT=w_words[:, w, :].bitcast(FP4X4),
@@ -167,59 +169,49 @@ def tile_l1regressionmoeactionhead_pa_t_kernel(
                     start=True,
                     stop=True,
                 )
-                acc_of[n, w] = acc
-
-        def multiply(n, w):
-            products = work.tile([P, 2, T], F32, name="products", bufs=4)
-            nc.vector.scalar_tensor_tensor(
-                out=products[:],
-                in0=acc_of[n, w][:].unsqueeze(1).to_broadcast([P, 2, T]),
-                scalar=per_feature[:, 2 + w : 3 + w],
-                in1=table[:],
-                op0=ALU.add,
-                op1=ALU.mult,
-            )
-            products_of[n, w] = products
+                biased = work.tile([P, T], F32, name="biased", bufs=4)
+                nc.scalar.activation(
+                    out=biased[:], in_=acc[:], func=ACT.Identity, bias=bias_of[:, w : w + 1]
+                )
+                biased_of[n, w] = biased
 
         def rotate_and_store(n):
+            backs = []
             for w in range(2):
-                products = products_of[n, w]
-                rotated = psum.tile([P, SUB, D], F32, name="rotated")
+                back = psum.tile([P, SUB, D], F32, name="back", bufs=4)
                 for c in range(SUB):
-                    tokens = slice(c * P, (c + 1) * P)
-                    nc.tensor.matmul(
-                        out=rotated[:, c, :],
-                        lhsT=products[:, 0, tokens],
-                        rhs=ident[:],
-                        is_transpose=True,
-                        start=True,
-                        stop=False,
+                    nc.tensor.transpose(
+                        back[:, c, :], biased_of[n, w][:, c * P : (c + 1) * P], ident[:]
                     )
-                    nc.tensor.matmul(
-                        out=rotated[:, c, :],
-                        lhsT=products[:, 1, tokens],
-                        rhs=swap[:],
-                        is_transpose=True,
-                        start=False,
-                        stop=True,
-                    )
+                backs.append(back)
+            for w in range(2):
+                products = work.tile([P, 2, SUB, D], F32, name="products", bufs=4)
+                nc.vector.tensor_tensor(
+                    out=products[:],
+                    in0=backs[w][:].unsqueeze(1).to_broadcast([P, 2, SUB, D]),
+                    in1=table[:],
+                    op=ALU.mult,
+                )
                 result = work.tile([P, SUB, D], F32, name="result", bufs=4)
-                nc.scalar.copy(out=result[:], in_=rotated[:])
+                nc.gpsimd.tensor_tensor(
+                    out=result[:].rearrange("p c (i e) -> p (c i) e", e=2),
+                    in0=products[:, 0].rearrange("p c (i e) -> p (c i) e", e=2),
+                    in1=products[:, 1].rearrange("p c (i e) -> p (c i) e", e=2)[:, :, ::-1],
+                    op=ALU.add,
+                )
                 nc.sync.dma_start(
                     out=outs[w][n, 0].rearrange("(p c) d -> p c d", c=SUB), in_=result[:]
                 )
 
         transpose_x(0)
         quantise(0)
-        nc.scalar.activation(out=table[:], in_=turns[:], func=ACT.Sin, scale=TWO_PI)
+        fill_tables()
         for n in range(BATCH):
             if n + 1 < BATCH:
                 transpose_x(n + 1)
             project(n)
-            multiply(n, 0)
             if n + 1 < BATCH:
                 quantise(n + 1)
-            multiply(n, 1)
             if n >= 1:
                 rotate_and_store(n - 1)
         rotate_and_store(BATCH - 1)

@@ -192,7 +192,7 @@ def tile_l1regressionmoeactionhead_pa_t_kernel(
                     in1=table[:],
                     op=ALU.mult,
                 )
-                result = work.tile([P, SUB, D], F32, name="result", bufs=4)
+                result = work.tile([P, SUB, D], F32, name="result", bufs=16)
                 nc.gpsimd.tensor_tensor(
                     out=result[:].rearrange("p c (i e) -> p (c i) e", e=2),
                     in0=products[:, 0].rearrange("p c (i e) -> p (c i) e", e=2),

@@ -68,8 +68,6 @@ def tile_l1regressionmoeactionhead_pa_t_kernel(
         nc.vector.memset(warm[:], 0.0)
         nc.scalar.activation(out=warm[:], in_=warm[:], func=ACT.Sin)
 
-        ident = keep.tile([P, P], F32)
-        masks.make_identity(nc, ident[:])
         position = keep.tile([P, SUB], F32)
         nc.gpsimd.iota(
             position[:],
@@ -78,13 +76,8 @@ def tile_l1regressionmoeactionhead_pa_t_kernel(
             channel_multiplier=SUB,
             allow_small_or_imprecise_dtypes=True,
         )
-
-        bias_rows_f32 = keep.tile([P, P], F32)
-        nc.vector.tensor_copy(out=bias_rows_f32[:], in_=bias_rows[:])
-        bias_columns = psum.tile([P, P], F32, tag="back", bufs=4)
-        nc.tensor.transpose(bias_columns[:], bias_rows_f32[:], ident[:])
-        bias_of = keep.tile([P, 2], F32)
-        nc.vector.tensor_copy(out=bias_of[:], in_=bias_columns[:, 0:2])
+        ident = keep.tile([P, P], F32)
+        masks.make_identity(nc, ident[:])
 
         pace = keep.tile([P, HALF], F32)
         ratio = ROPE_BASE ** (-1.0 / HALF)
@@ -128,6 +121,15 @@ def tile_l1regressionmoeactionhead_pa_t_kernel(
                     func=ACT.Sin,
                     scale=sign * TWO_PI,
                 )
+
+        fill_tables()
+
+        bias_rows_f32 = keep.tile([P, P], F32)
+        nc.vector.tensor_copy(out=bias_rows_f32[:], in_=bias_rows[:])
+        bias_columns = psum.tile([P, P], F32, tag="back", bufs=4)
+        nc.tensor.transpose(bias_columns[:], bias_rows_f32[:], ident[:])
+        bias_of = keep.tile([P, 2], F32)
+        nc.vector.tensor_copy(out=bias_of[:], in_=bias_columns[:, 0:2])
 
         grouped_of = {}
         codes_of = {}
@@ -204,14 +206,13 @@ def tile_l1regressionmoeactionhead_pa_t_kernel(
                 )
 
         transpose_x(0)
+        transpose_x(1)
         quantise(0)
-        fill_tables()
+        quantise(1)
         for n in range(BATCH):
-            if n + 1 < BATCH:
-                transpose_x(n + 1)
             project(n)
-            if n + 1 < BATCH:
-                quantise(n + 1)
-            if n >= 1:
-                rotate_and_store(n - 1)
-        rotate_and_store(BATCH - 1)
+            if n + 2 < BATCH:
+                transpose_x(n + 2)
+            rotate_and_store(n)
+            if n + 2 < BATCH:
+                quantise(n + 2)

@@ -43,26 +43,37 @@ def tile_l1regressionmoeactionhead_pa_t_kernel(
 
         x_sb = keep.tile([P, BATCH, SUB, K], BF16)
 
-        def load_x(n):
-            nc.sync.dma_start(out=x_sb[:, n], in_=x[n].rearrange("(p c) k -> p c k", c=SUB))
-
-        load_x(0)
+        def load_x(n, queue):
+            queue.dma_start(out=x_sb[:, n], in_=x[n].rearrange("(p c) k -> p c k", c=SUB))
 
         w_words = keep.tile([P, 2, 2 * D], U8, align_bytes=64)
         w_scales = keep.tile([P, 2, D], U8, align_bytes=64)
-        bias_rows = keep.tile([P, P], BF16)
         nc.vector.memset(w_scales[:].bitcast(I32), 0)
-        nc.vector.memset(bias_rows[:], 0.0)
-        for w, (words, scales, bias) in enumerate(weights):
+
+        def load_weight(w):
+            words, scales, bias = weights[w]
             nc.sync.dma_start(out=w_words[:, w, :].bitcast(I32), in_=words[0].bitcast(I32))
             for q in range(4):
                 nc.sync.dma_start(
                     out=w_scales[32 * q : 32 * q + 4, w, :].bitcast(I32),
                     in_=scales[0, 4 * q : 4 * q + 4, :].bitcast(I32),
                 )
-            nc.scalar.dma_start(out=bias_rows[w : w + 1, :], in_=bias.unsqueeze(0))
-        for n in range(1, BATCH):
-            load_x(n)
+
+        bias_of = []
+
+        def load_bias(w):
+            bias_column = keep.tile([P, 1], BF16, name="bias_column_%d" % w)
+            nc.sync.dma_start(out=bias_column[:], in_=weights[w][2].rearrange("(p o) -> p o", o=1))
+            bias_of.append(bias_column)
+
+        load_x(0, nc.scalar)
+        load_weight(0)
+        load_bias(0)
+        load_x(1, nc.scalar)
+        load_weight(1)
+        load_bias(1)
+        for n in range(2, BATCH):
+            load_x(n, nc.sync)
 
         warm = keep.tile([P, 1], F32)
         nc.vector.memset(warm[:], 0.0)
@@ -79,25 +90,33 @@ def tile_l1regressionmoeactionhead_pa_t_kernel(
         ident = keep.tile([P, P], F32)
         masks.make_identity(nc, ident[:])
 
-        pace = keep.tile([P, HALF], F32)
+        one = keep.tile([P, 1], F32)
+        nc.vector.memset(one[:], 1.0)
+        pace = keep.tile([P, 2, HALF], F32)
         ratio = ROPE_BASE ** (-1.0 / HALF)
-        nc.vector.memset(pace[:, 0:1], 1.0)
-        for doubling in range(6):
-            width = 2**doubling
-            nc.vector.tensor_scalar_mul(
-                out=pace[:, width : 2 * width], in0=pace[:, 0:width], scalar1=ratio**width
-            )
-        nc.vector.tensor_scalar_mul(out=pace[:], in0=pace[:], scalar1=1.0 / TWO_PI)
+        first = ((1.0, ratio, ratio**2, ratio**3), (ratio, -1.0, ratio**3, -(ratio**2)))
+        for s in range(2):
+            for j in range(4):
+                nc.vector.tensor_scalar_mul(
+                    out=pace[:, s, j : j + 1], in0=one[:], scalar1=first[s][j] / TWO_PI
+                )
+        for width in (4, 16):
+            for k in range(1, 4):
+                nc.vector.tensor_scalar_mul(
+                    out=pace[:, :, k * width : (k + 1) * width],
+                    in0=pace[:, :, 0:width],
+                    scalar1=ratio ** (k * width),
+                )
 
         turns = keep.tile([P, 2, SUB, HALF], F32)
         whole = keep.tile([P, 2, SUB, HALF], F32)
         nc.vector.tensor_tensor(
-            out=turns[:, 1],
-            in0=position[:].unsqueeze(2).to_broadcast([P, SUB, HALF]),
-            in1=pace[:].unsqueeze(1).to_broadcast([P, SUB, HALF]),
+            out=turns[:],
+            in0=position[:].unsqueeze(1).unsqueeze(3).to_broadcast([P, 2, SUB, HALF]),
+            in1=pace[:].unsqueeze(2).to_broadcast([P, 2, SUB, HALF]),
             op=ALU.mult,
         )
-        nc.vector.tensor_scalar_add(out=turns[:, 0], in0=turns[:, 1], scalar1=0.25)
+        nc.vector.tensor_scalar_add(out=turns[:, 0], in0=turns[:, 0], scalar1=0.25)
         nc.vector.tensor_scalar(
             out=whole[:], in0=turns[:], scalar1=ROUND, scalar2=ROUND, op0=ALU.add, op1=ALU.subtract
         )
@@ -107,46 +126,37 @@ def tile_l1regressionmoeactionhead_pa_t_kernel(
 
         def fill_tables():
             nc.scalar.activation(
-                out=table[:, 0].rearrange("p c (h j) -> p c h j", h=2),
-                in_=turns[:, 0].unsqueeze(2).to_broadcast([P, SUB, 2, HALF]),
+                out=table[:].rearrange("p s c (h j) -> p (s c) h j", h=2),
+                in_=turns[:]
+                .rearrange("p s c j -> p (s c) j")
+                .unsqueeze(2)
+                .to_broadcast([P, 2 * SUB, 2, HALF]),
                 func=ACT.Sin,
                 scale=TWO_PI,
             )
-            to_partner = table[:, 1].rearrange("p c (h i e) -> p c h i e", h=2, e=2)
-            angle_pairs = turns[:, 1].rearrange("p c (i e) -> p c i e", e=2)
-            for e, sign in enumerate((1.0, -1.0)):
-                nc.scalar.activation(
-                    out=to_partner[:, :, :, :, e],
-                    in_=angle_pairs[:, :, :, 1 - e].unsqueeze(2).to_broadcast([P, SUB, 2, HALF // 2]),
-                    func=ACT.Sin,
-                    scale=sign * TWO_PI,
-                )
 
-        fill_tables()
-
-        bias_rows_f32 = keep.tile([P, P], F32)
-        nc.vector.tensor_copy(out=bias_rows_f32[:], in_=bias_rows[:])
-        bias_columns = psum.tile([P, P], F32, tag="back", bufs=4)
-        nc.tensor.transpose(bias_columns[:], bias_rows_f32[:], ident[:])
-        bias_of = keep.tile([P, 2], F32)
-        nc.vector.tensor_copy(out=bias_of[:], in_=bias_columns[:, 0:2])
-
+        xt_of = {}
         grouped_of = {}
         codes_of = {}
         biased_of = {}
 
         def transpose_x(n):
-            grouped = work.tile([P, T * 4], BF16, align_bytes=64, name="grouped")
-            grouped_words = grouped[:].bitcast(F32).rearrange("p (c t u) -> p c t u", c=SUB, u=2)
+            xt_of[n] = []
             for h in range(SUB // 2):
                 xt = psum.tile([P, 2, 2, P], F32, name="xt")
                 for c in range(2):
                     x_words = x_sb[:, n, 2 * h + c, :].bitcast(F32)
                     for u in range(2):
                         nc.tensor.transpose(xt[:, c, u, :], x_words[:, u : K // 2 : 2], ident[:])
+                xt_of[n].append(xt)
+
+        def copy_x(n):
+            grouped = work.tile([P, T * 4], BF16, align_bytes=64, name="grouped")
+            grouped_words = grouped[:].bitcast(F32).rearrange("p (c t u) -> p c t u", c=SUB, u=2)
+            for h in range(SUB // 2):
                 nc.scalar.copy(
                     out=grouped_words[:, 2 * h : 2 * h + 2],
-                    in_=xt[:].rearrange("p c u t -> p c t u"),
+                    in_=xt_of[n][h][:].rearrange("p c u t -> p c t u"),
                 )
             grouped_of[n] = grouped
 
@@ -158,61 +168,75 @@ def tile_l1regressionmoeactionhead_pa_t_kernel(
             )
             codes_of[n] = (codes, plane)
 
-        def project(n):
+        def project(n, w):
             codes, plane = codes_of[n]
-            for w in range(2):
-                acc = psum.tile([P, T], F32, name="acc")
-                nc.tensor.matmul_mx(
-                    out=acc[:],
-                    lhsT=w_words[:, w, :].bitcast(FP4X4),
-                    lhsT_scale=w_scales[:, w, :],
-                    rhs=codes[:].bitcast(FP8X4),
-                    rhs_scale=plane[:],
-                    start=True,
-                    stop=True,
-                )
-                biased = work.tile([P, T], F32, name="biased", bufs=4)
-                nc.scalar.activation(
-                    out=biased[:], in_=acc[:], func=ACT.Identity, bias=bias_of[:, w : w + 1]
-                )
-                biased_of[n, w] = biased
+            acc = psum.tile([P, T], F32, name="acc")
+            nc.tensor.matmul_mx(
+                out=acc[:],
+                lhsT=w_words[:, w, :].bitcast(FP4X4),
+                lhsT_scale=w_scales[:, w, :],
+                rhs=codes[:].bitcast(FP8X4),
+                rhs_scale=plane[:],
+                start=True,
+                stop=True,
+            )
+            biased = work.tile([P, T], F32, name="biased", bufs=4)
+            nc.scalar.activation(
+                out=biased[:], in_=acc[:], func=ACT.Identity, bias=bias_of[w][:]
+            )
+            biased_of[n, w] = biased
 
-        def rotate_and_store(n):
-            backs = []
-            for w in range(2):
-                back = psum.tile([P, SUB, D], F32, name="back", bufs=4)
-                for c in range(SUB):
-                    nc.tensor.transpose(
-                        back[:, c, :], biased_of[n, w][:, c * P : (c + 1) * P], ident[:]
-                    )
-                backs.append(back)
-            for w in range(2):
-                products = work.tile([P, 2, SUB, D], F32, name="products", bufs=4)
+        def rotate_and_store(n, w, pieces=((0, SUB, nc.gpsimd),)):
+            back = psum.tile([P, SUB, D], F32, name="back", bufs=4)
+            for c in range(SUB):
+                nc.tensor.transpose(
+                    back[:, c, :], biased_of[n, w][:, c * P : (c + 1) * P], ident[:]
+                )
+            products = work.tile([P, 2, SUB, D], F32, name="products", bufs=4)
+            result = work.tile([P, SUB, D], F32, name="result", bufs=16)
+            for c0, c1, adder in pieces:
                 nc.vector.tensor_tensor(
-                    out=products[:],
-                    in0=backs[w][:].unsqueeze(1).to_broadcast([P, 2, SUB, D]),
-                    in1=table[:],
+                    out=products[:, :, c0:c1],
+                    in0=back[:, c0:c1].unsqueeze(1).to_broadcast([P, 2, c1 - c0, D]),
+                    in1=table[:, :, c0:c1],
                     op=ALU.mult,
                 )
-                result = work.tile([P, SUB, D], F32, name="result", bufs=16)
-                nc.gpsimd.tensor_tensor(
-                    out=result[:].rearrange("p c (i e) -> p (c i) e", e=2),
-                    in0=products[:, 0].rearrange("p c (i e) -> p (c i) e", e=2),
-                    in1=products[:, 1].rearrange("p c (i e) -> p (c i) e", e=2)[:, :, ::-1],
+            for c0, c1, adder in pieces:
+                adder.tensor_tensor(
+                    out=result[:, c0:c1].rearrange("p c (i e) -> p (c i) e", e=2),
+                    in0=products[:, 0, c0:c1].rearrange("p c (i e) -> p (c i) e", e=2),
+                    in1=products[:, 1, c0:c1].rearrange("p c (i e) -> p (c i) e", e=2)[:, :, ::-1],
                     op=ALU.add,
                 )
                 nc.sync.dma_start(
-                    out=outs[w][n, 0].rearrange("(p c) d -> p c d", c=SUB), in_=result[:]
+                    out=outs[w][n, 0].rearrange("(p c) d -> p c d", c=SUB)[:, c0:c1],
+                    in_=result[:, c0:c1],
                 )
 
         transpose_x(0)
-        transpose_x(1)
+        copy_x(0)
+        fill_tables()
         quantise(0)
+        transpose_x(1)
+        project(0, 0)
+        copy_x(1)
+        project(0, 1)
+        rotate_and_store(0, 0)
         quantise(1)
-        for n in range(BATCH):
-            project(n)
+        transpose_x(2)
+        copy_x(2)
+        rotate_and_store(0, 1)
+        quantise(2)
+        for n in range(1, BATCH):
+            project(n, 0)
+            project(n, 1)
             if n + 2 < BATCH:
                 transpose_x(n + 2)
-            rotate_and_store(n)
+                copy_x(n + 2)
+            rotate_and_store(n, 0)
+            if n + 1 < BATCH:
+                rotate_and_store(n, 1)
+            else:
+                rotate_and_store(n, 1, ((0, SUB // 2, nc.vector), (SUB // 2, SUB, nc.vector)))
             if n + 2 < BATCH:
                 quantise(n + 2)

@@ -150,11 +150,11 @@ def tile_l1regressionmoeactionhead_pa_t_kernel(
                         nc.tensor.transpose(xt[:, c, u, :], x_words[:, u : K // 2 : 2], ident[:])
                 xt_of[n].append(xt)
 
-        def copy_x(n):
+        def copy_x(n, copy=nc.scalar.copy):
             grouped = work.tile([P, T * 4], BF16, align_bytes=64, name="grouped")
             grouped_words = grouped[:].bitcast(F32).rearrange("p (c t u) -> p c t u", c=SUB, u=2)
             for h in range(SUB // 2):
-                nc.scalar.copy(
+                copy(
                     out=grouped_words[:, 2 * h : 2 * h + 2],
                     in_=xt_of[n][h][:].rearrange("p c u t -> p c t u"),
                 )
@@ -219,10 +219,10 @@ def tile_l1regressionmoeactionhead_pa_t_kernel(
         quantise(0)
         transpose_x(1)
         project(0, 0)
-        copy_x(1)
+        copy_x(1, nc.vector.tensor_copy)
+        quantise(1)
         project(0, 1)
         rotate_and_store(0, 0)
-        quantise(1)
         transpose_x(2)
         copy_x(2)
         rotate_and_store(0, 1)

@@ -139,6 +139,7 @@ def tile_l1regressionmoeactionhead_pa_t_kernel(
         grouped_of = {}
         codes_of = {}
         biased_of = {}
+        back_of = {}
 
         def transpose_x(n):
             xt_of[n] = []
@@ -186,31 +187,40 @@ def tile_l1regressionmoeactionhead_pa_t_kernel(
             )
             biased_of[n, w] = biased
 
-        def rotate_and_store(n, w, pieces=((0, SUB, nc.gpsimd),)):
-            back = psum.tile([P, SUB, D], F32, name="back", bufs=4)
-            for c in range(SUB):
-                nc.tensor.transpose(
-                    back[:, c, :], biased_of[n, w][:, c * P : (c + 1) * P], ident[:]
-                )
-            products = work.tile([P, 2, SUB, D], F32, name="products", bufs=4)
-            result = work.tile([P, SUB, D], F32, name="result", bufs=16)
-            for c0, c1, adder in pieces:
-                nc.vector.tensor_tensor(
-                    out=products[:, :, c0:c1],
-                    in0=back[:, c0:c1].unsqueeze(1).to_broadcast([P, 2, c1 - c0, D]),
-                    in1=table[:, :, c0:c1],
-                    op=ALU.mult,
-                )
-            for c0, c1, adder in pieces:
-                adder.tensor_tensor(
-                    out=result[:, c0:c1].rearrange("p c (i e) -> p (c i) e", e=2),
-                    in0=products[:, 0, c0:c1].rearrange("p c (i e) -> p (c i) e", e=2),
-                    in1=products[:, 1, c0:c1].rearrange("p c (i e) -> p (c i) e", e=2)[:, :, ::-1],
-                    op=ALU.add,
-                )
+        products_of = {}
+        result_of = {}
+
+        def multiply(n, w, c0=0, c1=SUB):
+            if (n, w) not in back_of:
+                back = psum.tile([P, SUB, D], F32, name="back", bufs=4)
+                for c in range(SUB):
+                    nc.tensor.transpose(
+                        back[:, c, :], biased_of[n, w][:, c * P : (c + 1) * P], ident[:]
+                    )
+                back_of[n, w] = back
+            if n not in products_of:
+                products_of[n] = work.tile([P, 2, 2, SUB, D], F32, name="products", bufs=3)
+                result_of[n] = work.tile([P, 2, SUB, D], F32, name="result", bufs=8)
+            nc.vector.tensor_tensor(
+                out=products_of[n][:, w, :, c0:c1],
+                in0=back_of[n, w][:, c0:c1].unsqueeze(1).to_broadcast([P, 2, c1 - c0, D]),
+                in1=table[:, :, c0:c1],
+                op=ALU.mult,
+            )
+
+        def add_and_store(n, adder, w0=0, w1=2, c0=0, c1=SUB):
+            adder.tensor_tensor(
+                out=result_of[n][:, w0:w1, c0:c1].rearrange("p w c (i e) -> p w (c i) e", e=2),
+                in0=products_of[n][:, w0:w1, 0, c0:c1].rearrange("p w c (i e) -> p w (c i) e", e=2),
+                in1=products_of[n][:, w0:w1, 1, c0:c1].rearrange("p w c (i e) -> p w (c i) e", e=2)[
+                    :, :, :, ::-1
+                ],
+                op=ALU.add,
+            )
+            for w in range(w0, w1):
                 nc.sync.dma_start(
                     out=outs[w][n, 0].rearrange("(p c) d -> p c d", c=SUB)[:, c0:c1],
-                    in_=result[:, c0:c1],
+                    in_=result_of[n][:, w, c0:c1],
                 )
 
         transpose_x(0)
@@ -222,21 +232,33 @@ def tile_l1regressionmoeactionhead_pa_t_kernel(
         copy_x(1, nc.vector.tensor_copy)
         quantise(1)
         project(0, 1)
-        rotate_and_store(0, 0)
+        multiply(0, 0)
         transpose_x(2)
         copy_x(2)
-        rotate_and_store(0, 1)
+        multiply(0, 1)
+        add_and_store(0, nc.gpsimd)
         quantise(2)
-        for n in range(1, BATCH):
+        for n in range(1, BATCH - 1):
             project(n, 0)
             project(n, 1)
             if n + 2 < BATCH:
                 transpose_x(n + 2)
                 copy_x(n + 2)
-            rotate_and_store(n, 0)
-            if n + 1 < BATCH:
-                rotate_and_store(n, 1)
-            else:
-                rotate_and_store(n, 1, ((0, SUB // 2, nc.vector), (SUB // 2, SUB, nc.vector)))
+            multiply(n, 0)
             if n + 2 < BATCH:
+                multiply(n, 1)
+                add_and_store(n, nc.gpsimd)
                 quantise(n + 2)
+            else:
+                add_and_store(n, nc.gpsimd, 0, 1)
+                multiply(n, 1)
+                add_and_store(n, nc.gpsimd, 1, 2)
+        last = BATCH - 1
+        project(last, 0)
+        project(last, 1)
+        multiply(last, 0)
+        add_and_store(last, nc.gpsimd, 0, 1)
+        multiply(last, 1, 0, SUB // 2)
+        multiply(last, 1, SUB // 2, SUB)
+        add_and_store(last, nc.vector, 1, 2, 0, SUB // 2)
+        add_and_store(last, nc.vector, 1, 2, SUB // 2, SUB)

@@ -245,20 +245,15 @@ def tile_l1regressionmoeactionhead_pa_t_kernel(
                 transpose_x(n + 2)
                 copy_x(n + 2)
             multiply(n, 0)
+            multiply(n, 1)
+            add_and_store(n, nc.gpsimd)
             if n + 2 < BATCH:
-                multiply(n, 1)
-                add_and_store(n, nc.gpsimd)
                 quantise(n + 2)
-            else:
-                add_and_store(n, nc.gpsimd, 0, 1)
-                multiply(n, 1)
-                add_and_store(n, nc.gpsimd, 1, 2)
         last = BATCH - 1
         project(last, 0)
         project(last, 1)
         multiply(last, 0)
-        add_and_store(last, nc.gpsimd, 0, 1)
-        multiply(last, 1, 0, SUB // 2)
-        multiply(last, 1, SUB // 2, SUB)
+        multiply(last, 1)
+        add_and_store(last, nc.vector, 0, 1)
         add_and_store(last, nc.vector, 1, 2, 0, SUB // 2)
         add_and_store(last, nc.vector, 1, 2, SUB // 2, SUB)

@@ -25,6 +25,8 @@ ROPE_BASE = 10000.0
 TWO_PI = 2.0 * math.pi
 ROUND = 1.5 * 2.0**23
 
+WARM_UP = 5
+
 FLOPS = 2 * BATCH * T * K * 2 * D
 
 
@@ -49,6 +51,12 @@ def tile_l1regressionmoeactionhead_pa_t_kernel(
         w_words = keep.tile([P, 2, 2 * D], U8, align_bytes=64)
         w_scales = keep.tile([P, 2, D], U8, align_bytes=64)
         nc.vector.memset(w_scales[:].bitcast(I32), 0)
+
+        idle = keep.tile([P, T], BF16)
+        nc.vector.memset(idle[:], 0.0)
+        unused = psum.tile([P, T], F32, name="acc")
+        for repeat in range(WARM_UP):
+            nc.tensor.matmul(out=unused[:], lhsT=idle[:, 0:P], rhs=idle[:], start=True, stop=True)
 
         def load_weight(w):
             words, scales, bias = weights[w]

@@ -25,7 +25,7 @@ ROPE_BASE = 10000.0
 TWO_PI = 2.0 * math.pi
 ROUND = 1.5 * 2.0**23
 
-WARM_UP = 5
+WARM_UP = 3
 
 FLOPS = 2 * BATCH * T * K * 2 * D
 
@@ -45,18 +45,28 @@ def tile_l1regressionmoeactionhead_pa_t_kernel(
 
         x_sb = keep.tile([P, BATCH, SUB, K], BF16)
 
-        def load_x(n, queue):
-            queue.dma_start(out=x_sb[:, n], in_=x[n].rearrange("(p c) k -> p c k", c=SUB))
+        def load_x(n, queue, c0=0, c1=SUB):
+            queue.dma_start(
+                out=x_sb[:, n, c0:c1], in_=x[n].rearrange("(p c) k -> p c k", c=SUB)[:, c0:c1]
+            )
 
         w_words = keep.tile([P, 2, 2 * D], U8, align_bytes=64)
         w_scales = keep.tile([P, 2, D], U8, align_bytes=64)
         nc.vector.memset(w_scales[:].bitcast(I32), 0)
 
-        idle = keep.tile([P, T], BF16)
+        idle = keep.tile([P, P], BF16)
         nc.vector.memset(idle[:], 0.0)
+        one = keep.tile([P, 1], F32)
+        nc.vector.memset(one[:], 1.0)
         unused = psum.tile([P, T], F32, name="acc")
         for repeat in range(WARM_UP):
-            nc.tensor.matmul(out=unused[:], lhsT=idle[:, 0:P], rhs=idle[:], start=True, stop=True)
+            nc.tensor.matmul(
+                out=unused[:],
+                lhsT=idle[:],
+                rhs=idle[:, 0:1].to_broadcast([P, T]),
+                start=True,
+                stop=True,
+            )
 
         def load_weight(w):
             words, scales, bias = weights[w]
@@ -71,21 +81,20 @@ def tile_l1regressionmoeactionhead_pa_t_kernel(
 
         def load_bias(w):
             bias_column = keep.tile([P, 1], BF16, name="bias_column_%d" % w)
-            nc.sync.dma_start(out=bias_column[:], in_=weights[w][2].rearrange("(p o) -> p o", o=1))
+            nc.gpsimd.dma_start(out=bias_column[:], in_=weights[w][2].rearrange("(p o) -> p o", o=1))
             bias_of.append(bias_column)
 
-        load_x(0, nc.scalar)
+        load_x(0, nc.scalar, 0, SUB // 2)
+        load_x(0, nc.scalar, SUB // 2, SUB)
         load_weight(0)
-        load_bias(0)
         load_x(1, nc.scalar)
+        load_x(2, nc.sync)
         load_weight(1)
-        load_bias(1)
-        for n in range(2, BATCH):
+        for n in range(3, BATCH):
             load_x(n, nc.sync)
 
         warm = keep.tile([P, 1], F32)
-        nc.vector.memset(warm[:], 0.0)
-        nc.scalar.activation(out=warm[:], in_=warm[:], func=ACT.Sin)
+        nc.scalar.activation(out=warm[:], in_=one[:], func=ACT.Sin)
 
         position = keep.tile([P, SUB], F32)
         nc.gpsimd.iota(
@@ -97,9 +106,9 @@ def tile_l1regressionmoeactionhead_pa_t_kernel(
         )
         ident = keep.tile([P, P], F32)
         masks.make_identity(nc, ident[:])
+        load_bias(0)
+        load_bias(1)
 
-        one = keep.tile([P, 1], F32)
-        nc.vector.memset(one[:], 1.0)
         pace = keep.tile([P, 2, HALF], F32)
         ratio = ROPE_BASE ** (-1.0 / HALF)
         first = ((1.0, ratio, ratio**2, ratio**3), (ratio, -1.0, ratio**3, -(ratio**2)))
@@ -130,15 +139,12 @@ def tile_l1regressionmoeactionhead_pa_t_kernel(
         )
         nc.vector.tensor_sub(out=turns[:], in0=turns[:], in1=whole[:])
 
-        table = keep.tile([P, 2, SUB, D], F32)
+        table = keep.tile([P, SUB, 2, HALF], F32)
 
         def fill_tables():
             nc.scalar.activation(
-                out=table[:].rearrange("p s c (h j) -> p (s c) h j", h=2),
-                in_=turns[:]
-                .rearrange("p s c j -> p (s c) j")
-                .unsqueeze(2)
-                .to_broadcast([P, 2 * SUB, 2, HALF]),
+                out=table[:].rearrange("p c s j -> p s c j"),
+                in_=turns[:],
                 func=ACT.Sin,
                 scale=TWO_PI,
             )
@@ -146,82 +152,94 @@ def tile_l1regressionmoeactionhead_pa_t_kernel(
         xt_of = {}
         grouped_of = {}
         codes_of = {}
+        acc_of = {}
         biased_of = {}
         back_of = {}
 
-        def transpose_x(n):
-            xt_of[n] = []
-            for h in range(SUB // 2):
-                xt = psum.tile([P, 2, 2, P], F32, name="xt")
-                for c in range(2):
-                    x_words = x_sb[:, n, 2 * h + c, :].bitcast(F32)
-                    for u in range(2):
-                        nc.tensor.transpose(xt[:, c, u, :], x_words[:, u : K // 2 : 2], ident[:])
-                xt_of[n].append(xt)
+        def transpose_x(n, h):
+            xt = psum.tile([P, 2, 2, P], F32, name="xt")
+            for c in range(2):
+                x_words = x_sb[:, n, 2 * h + c, :].bitcast(F32)
+                for u in range(2):
+                    nc.tensor.transpose(xt[:, c, u, :], x_words[:, u : K // 2 : 2], ident[:])
+            xt_of[n, h] = xt
 
-        def copy_x(n, copy=nc.scalar.copy):
-            grouped = work.tile([P, T * 4], BF16, align_bytes=64, name="grouped")
-            grouped_words = grouped[:].bitcast(F32).rearrange("p (c t u) -> p c t u", c=SUB, u=2)
-            for h in range(SUB // 2):
-                copy(
-                    out=grouped_words[:, 2 * h : 2 * h + 2],
-                    in_=xt_of[n][h][:].rearrange("p c u t -> p c t u"),
-                )
-            grouped_of[n] = grouped
-
-        def quantise(n):
-            codes = work.tile([P, T], U32, align_bytes=64, name="codes")
-            plane = work.tile([P, T], U8, align_bytes=64, name="plane")
-            nc.vector.quantize_mx(
-                out=codes[:].bitcast(FP8X4), scales=plane[:], in_=grouped_of[n][:]
+        def copy_x(n, h, copy=nc.scalar.copy):
+            if n not in grouped_of:
+                grouped_of[n] = work.tile([P, T * 4], BF16, align_bytes=64, name="grouped")
+            words = grouped_of[n][:].bitcast(F32).rearrange("p (c t u) -> p c t u", c=SUB, u=2)
+            copy(
+                out=words[:, 2 * h : 2 * h + 2],
+                in_=xt_of[n, h][:].rearrange("p c u t -> p c t u"),
             )
-            codes_of[n] = (codes, plane)
 
-        def project(n, w):
+        def quantise(n, c0=0, c1=SUB):
+            if n not in codes_of:
+                codes = work.tile([P, T], U32, align_bytes=64, name="codes")
+                plane = work.tile([P, T], U8, align_bytes=64, name="plane")
+                codes_of[n] = (codes, plane)
+            codes, plane = codes_of[n]
+            nc.vector.quantize_mx(
+                out=codes[:, c0 * P : c1 * P].bitcast(FP8X4),
+                scales=plane[:, c0 * P : c1 * P],
+                in_=grouped_of[n][:, c0 * P * 4 : c1 * P * 4],
+            )
+
+        def project(n, w, c0=0, c1=SUB):
             codes, plane = codes_of[n]
             acc = psum.tile([P, T], F32, name="acc")
             nc.tensor.matmul_mx(
-                out=acc[:],
+                out=acc[:, c0 * P : c1 * P],
                 lhsT=w_words[:, w, :].bitcast(FP4X4),
                 lhsT_scale=w_scales[:, w, :],
-                rhs=codes[:].bitcast(FP8X4),
-                rhs_scale=plane[:],
+                rhs=codes[:, c0 * P : c1 * P].bitcast(FP8X4),
+                rhs_scale=plane[:, c0 * P : c1 * P],
                 start=True,
                 stop=True,
             )
-            biased = work.tile([P, T], F32, name="biased", bufs=4)
+            acc_of[n, w, c0] = acc
+
+        def add_bias(n, w, c0=0, c1=SUB):
+            if (n, w) not in biased_of:
+                biased_of[n, w] = work.tile([P, T], F32, name="biased", bufs=4)
             nc.scalar.activation(
-                out=biased[:], in_=acc[:], func=ACT.Identity, bias=bias_of[w][:]
+                out=biased_of[n, w][:, c0 * P : c1 * P],
+                in_=acc_of[n, w, c0][:, c0 * P : c1 * P],
+                func=ACT.Identity,
+                bias=bias_of[w][:],
             )
-            biased_of[n, w] = biased
+
+        def transpose_back(n, w, c0=0, c1=SUB):
+            back = psum.tile([P, SUB, D], F32, name="back", bufs=4)
+            for c in range(c0, c1):
+                nc.tensor.transpose(
+                    back[:, c, :], biased_of[n, w][:, c * P : (c + 1) * P], ident[:]
+                )
+            back_of[n, w, c0] = back
 
         products_of = {}
         result_of = {}
 
         def multiply(n, w, c0=0, c1=SUB):
-            if (n, w) not in back_of:
-                back = psum.tile([P, SUB, D], F32, name="back", bufs=4)
-                for c in range(SUB):
-                    nc.tensor.transpose(
-                        back[:, c, :], biased_of[n, w][:, c * P : (c + 1) * P], ident[:]
-                    )
-                back_of[n, w] = back
             if n not in products_of:
-                products_of[n] = work.tile([P, 2, 2, SUB, D], F32, name="products", bufs=3)
+                products_of[n] = work.tile([P, 2, SUB, 2, D], F32, name="products", bufs=3)
                 result_of[n] = work.tile([P, 2, SUB, D], F32, name="result", bufs=8)
             nc.vector.tensor_tensor(
-                out=products_of[n][:, w, :, c0:c1],
-                in0=back_of[n, w][:, c0:c1].unsqueeze(1).to_broadcast([P, 2, c1 - c0, D]),
-                in1=table[:, :, c0:c1],
+                out=products_of[n][:, w, c0:c1].rearrange("p c s (h j) -> p c s h j", h=2),
+                in0=back_of[n, w, c0][:, c0:c1]
+                .rearrange("p c (h j) -> p c h j", h=2)
+                .unsqueeze(2)
+                .to_broadcast([P, c1 - c0, 2, 2, HALF]),
+                in1=table[:, c0:c1].unsqueeze(3).to_broadcast([P, c1 - c0, 2, 2, HALF]),
                 op=ALU.mult,
             )
 
         def add_and_store(n, adder, w0=0, w1=2, c0=0, c1=SUB):
             adder.tensor_tensor(
-                out=result_of[n][:, w0:w1, c0:c1].rearrange("p w c (i e) -> p w (c i) e", e=2),
-                in0=products_of[n][:, w0:w1, 0, c0:c1].rearrange("p w c (i e) -> p w (c i) e", e=2),
-                in1=products_of[n][:, w0:w1, 1, c0:c1].rearrange("p w c (i e) -> p w (c i) e", e=2)[
-                    :, :, :, ::-1
+                out=result_of[n][:, w0:w1, c0:c1].rearrange("p w c (i e) -> p w c i e", e=2),
+                in0=products_of[n][:, w0:w1, c0:c1, 0].rearrange("p w c (i e) -> p w c i e", e=2),
+                in1=products_of[n][:, w0:w1, c0:c1, 1].rearrange("p w c (i e) -> p w c i e", e=2)[
+                    :, :, :, :, ::-1
                 ],
                 op=ALU.add,
             )
@@ -231,37 +249,57 @@ def tile_l1regressionmoeactionhead_pa_t_kernel(
                     in_=result_of[n][:, w, c0:c1],
                 )
 
-        transpose_x(0)
-        copy_x(0)
+        half = SUB // 2
+        transpose_x(0, 0)
+        transpose_x(0, 1)
+        copy_x(0, 0)
+        copy_x(0, 1)
         fill_tables()
-        quantise(0)
-        transpose_x(1)
-        project(0, 0)
-        copy_x(1, nc.vector.tensor_copy)
+        quantise(0, 0, half)
+        quantise(0, half, SUB)
+        transpose_x(1, 0)
+        project(0, 0, 0, half)
+        transpose_x(1, 1)
+        copy_x(1, 0, nc.vector.tensor_copy)
+        add_bias(0, 0, 0, half)
+        copy_x(1, 1)
+        project(0, 0, half, SUB)
+        add_bias(0, 0, half, SUB)
+        transpose_back(0, 0, 0, half)
+        multiply(0, 0, 0, half)
         quantise(1)
         project(0, 1)
-        multiply(0, 0)
-        transpose_x(2)
-        copy_x(2)
+        add_bias(0, 1)
+        transpose_back(0, 0, half, SUB)
+        multiply(0, 0, half, SUB)
+        for h in range(2):
+            transpose_x(2, h)
+            copy_x(2, h)
+        transpose_back(0, 1)
         multiply(0, 1)
         add_and_store(0, nc.gpsimd)
         quantise(2)
         for n in range(1, BATCH - 1):
-            project(n, 0)
-            project(n, 1)
+            for w in range(2):
+                project(n, w)
+                add_bias(n, w)
             if n + 2 < BATCH:
-                transpose_x(n + 2)
-                copy_x(n + 2)
-            multiply(n, 0)
-            multiply(n, 1)
+                for h in range(2):
+                    transpose_x(n + 2, h)
+                    copy_x(n + 2, h)
+            for w in range(2):
+                transpose_back(n, w)
+                multiply(n, w)
             add_and_store(n, nc.gpsimd)
             if n + 2 < BATCH:
                 quantise(n + 2)
         last = BATCH - 1
-        project(last, 0)
-        project(last, 1)
-        multiply(last, 0)
-        multiply(last, 1)
+        for w in range(2):
+            project(last, w)
+            add_bias(last, w)
+        for w in range(2):
+            transpose_back(last, w)
+            multiply(last, w)
         add_and_store(last, nc.vector, 0, 1)
         add_and_store(last, nc.vector, 1, 2, 0, SUB // 2)
         add_and_store(last, nc.vector, 1, 2, SUB // 2, SUB)

@@ -149,6 +149,28 @@ def tile_l1regressionmoeactionhead_pa_t_kernel(
                 scale=TWO_PI,
             )
 
+        wide_table = keep.tile([P, SUB, 2, D], F32)
+        turned_table = keep.tile([P, 2, SUB, P], F32)
+        swap = keep.tile([P, P], F32)
+
+        def widen_table(c0, c1):
+            nc.scalar.copy(
+                out=wide_table[:, c0:c1].rearrange("p c s (h j) -> p c s h j", h=2),
+                in_=table[:, c0:c1].unsqueeze(3).to_broadcast([P, c1 - c0, 2, 2, HALF]),
+            )
+
+        def turn_table(s):
+            bank = psum.tile([P, SUB, P], F32, name="back", bufs=4)
+            for c in range(SUB):
+                nc.tensor.transpose(bank[:, c, :], wide_table[:, c, s, :], ident[:])
+            nc.scalar.copy(out=turned_table[:, s], in_=bank[:])
+
+        def make_swap():
+            nc.scalar.copy(
+                out=swap[:].rearrange("p (i e) -> p i e", e=2),
+                in_=ident[:].rearrange("p (i e) -> p i e", e=2)[:, :, ::-1],
+            )
+
         xt_of = {}
         grouped_of = {}
         codes_of = {}
@@ -185,9 +207,9 @@ def tile_l1regressionmoeactionhead_pa_t_kernel(
                 in_=grouped_of[n][:, c0 * P * 4 : c1 * P * 4],
             )
 
-        def project(n, w, c0=0, c1=SUB):
+        def project(n, w, c0=0, c1=SUB, name="acc"):
             codes, plane = codes_of[n]
-            acc = psum.tile([P, T], F32, name="acc")
+            acc = psum.tile([P, T], F32, name=name)
             nc.tensor.matmul_mx(
                 out=acc[:, c0 * P : c1 * P],
                 lhsT=w_words[:, w, :].bitcast(FP4X4),
@@ -219,10 +241,12 @@ def tile_l1regressionmoeactionhead_pa_t_kernel(
 
         products_of = {}
         result_of = {}
+        turned_of = {}
 
         def multiply(n, w, c0=0, c1=SUB):
             if n not in products_of:
                 products_of[n] = work.tile([P, 2, SUB, 2, D], F32, name="products", bufs=3)
+            if n not in result_of:
                 result_of[n] = work.tile([P, 2, SUB, D], F32, name="result", bufs=8)
             nc.vector.tensor_tensor(
                 out=products_of[n][:, w, c0:c1].rearrange("p c s (h j) -> p c s h j", h=2),
@@ -248,6 +272,38 @@ def tile_l1regressionmoeactionhead_pa_t_kernel(
                     out=outs[w][n, 0].rearrange("(p c) d -> p c d", c=SUB)[:, c0:c1],
                     in_=result_of[n][:, w, c0:c1],
                 )
+
+        def multiply_turned(n, w, c0, c1):
+            turned = work.tile([P, 2, SUB, P], F32, name="turned")
+            for s in range(2):
+                nc.vector.scalar_tensor_tensor(
+                    out=turned[:, s, c0:c1],
+                    in0=acc_of[n, w, c0][:, c0 * P : c1 * P].rearrange("p (c t) -> p c t", t=P),
+                    scalar=bias_of[w][:],
+                    in1=turned_table[:, s, c0:c1],
+                    op0=ALU.add,
+                    op1=ALU.mult,
+                )
+            turned_of[n, w, c0] = turned
+
+        def sum_and_store(n, w, c0, c1):
+            turned = turned_of[n, w, c0]
+            bank = psum.tile([P, SUB, D], F32, name="back", bufs=4)
+            for c in range(c0, c1):
+                for s, columns in ((0, ident), (1, swap)):
+                    nc.tensor.matmul(
+                        out=bank[:, c, :],
+                        lhsT=turned[:, s, c, :],
+                        rhs=columns[:],
+                        is_transpose=True,
+                        start=(s == 0),
+                        stop=(s == 1),
+                    )
+            nc.scalar.copy(out=result_of[n][:, w, c0:c1], in_=bank[:, c0:c1])
+            nc.sync.dma_start(
+                out=outs[w][n, 0].rearrange("(p c) d -> p c d", c=SUB)[:, c0:c1],
+                in_=result_of[n][:, w, c0:c1],
+            )
 
         half = SUB // 2
         transpose_x(0, 0)
@@ -279,27 +335,43 @@ def tile_l1regressionmoeactionhead_pa_t_kernel(
         multiply(0, 1)
         add_and_store(0, nc.gpsimd)
         quantise(2)
-        for n in range(1, BATCH - 1):
+        for n in range(1, BATCH - 2):
             for w in range(2):
                 project(n, w)
                 add_bias(n, w)
-            if n + 2 < BATCH:
-                for h in range(2):
-                    transpose_x(n + 2, h)
-                    copy_x(n + 2, h)
+            for h in range(2):
+                transpose_x(n + 2, h)
+                copy_x(n + 2, h)
             for w in range(2):
                 transpose_back(n, w)
                 multiply(n, w)
             add_and_store(n, nc.gpsimd)
-            if n + 2 < BATCH:
-                quantise(n + 2)
+            quantise(n + 2)
+            if n == 4:
+                make_swap()
+                widen_table(0, half)
+            if n == 5:
+                widen_table(half, SUB)
+            if n in (6, 7):
+                turn_table(n - 6)
         last = BATCH - 1
-        for w in range(2):
-            project(last, w)
-            add_bias(last, w)
-        for w in range(2):
-            transpose_back(last, w)
-            multiply(last, w)
-        add_and_store(last, nc.vector, 0, 1)
-        add_and_store(last, nc.vector, 1, 2, 0, SUB // 2)
-        add_and_store(last, nc.vector, 1, 2, SUB // 2, SUB)
+        project(last - 1, 0)
+        add_bias(last - 1, 0)
+        project(last - 1, 1, name="xt")
+        transpose_back(last - 1, 0)
+        multiply(last - 1, 0)
+        add_and_store(last - 1, nc.gpsimd, 0, 1)
+        multiply_turned(last - 1, 1, 0, SUB)
+        result_of[last] = work.tile([P, 2, SUB, D], F32, name="result", bufs=8)
+        project(last, 1, 0, half)
+        add_bias(last, 1, 0, half)
+        project(last, 0, name="xt")
+        project(last, 1, half, SUB)
+        transpose_back(last, 1, 0, half)
+        sum_and_store(last - 1, 1, 0, SUB)
+        multiply_turned(last, 0, 0, SUB)
+        sum_and_store(last, 0, 0, SUB)
+        multiply_turned(last, 1, half, SUB)
+        sum_and_store(last, 1, half, SUB)
+        multiply(last, 1, 0, half)
+        add_and_store(last, nc.vector, 1, 2, 0, half)

@@ -58,15 +58,19 @@ def tile_l1regressionmoeactionhead_pa_t_kernel(
         nc.vector.memset(idle[:], 0.0)
         one = keep.tile([P, 1], F32)
         nc.vector.memset(one[:], 1.0)
-        unused = psum.tile([P, T], F32, name="acc")
-        for repeat in range(WARM_UP):
-            nc.tensor.matmul(
-                out=unused[:],
-                lhsT=idle[:],
-                rhs=idle[:, 0:1].to_broadcast([P, T]),
-                start=True,
-                stop=True,
-            )
+        unused = psum.tile([P, T], F32, name="back", bufs=4)
+
+        def keep_warm(passes):
+            for repeat in range(passes):
+                nc.tensor.matmul(
+                    out=unused[:],
+                    lhsT=idle[:],
+                    rhs=idle[:, 0:1].to_broadcast([P, T]),
+                    start=True,
+                    stop=True,
+                )
+
+        keep_warm(WARM_UP)
 
         def load_weight(w):
             words, scales, bias = weights[w]
@@ -308,6 +312,7 @@ def tile_l1regressionmoeactionhead_pa_t_kernel(
         half = SUB // 2
         transpose_x(0, 0)
         transpose_x(0, 1)
+        keep_warm(2)
         copy_x(0, 0)
         copy_x(0, 1)
         fill_tables()
@@ -320,11 +325,13 @@ def tile_l1regressionmoeactionhead_pa_t_kernel(
         add_bias(0, 0, 0, half)
         copy_x(1, 1)
         project(0, 0, half, SUB)
+        keep_warm(1)
         add_bias(0, 0, half, SUB)
         transpose_back(0, 0, 0, half)
         multiply(0, 0, 0, half)
         quantise(1)
         project(0, 1)
+        keep_warm(1)
         add_bias(0, 1)
         transpose_back(0, 0, half, SUB)
         multiply(0, 0, half, SUB)

@@ -25,7 +25,7 @@ ROPE_BASE = 10000.0
 TWO_PI = 2.0 * math.pi
 ROUND = 1.5 * 2.0**23
 
-WARM_UP = 3
+WARM_UP = 4
 
 FLOPS = 2 * BATCH * T * K * 2 * D
 
@@ -58,9 +58,8 @@ def tile_l1regressionmoeactionhead_pa_t_kernel(
         nc.vector.memset(idle[:], 0.0)
         one = keep.tile([P, 1], F32)
         nc.vector.memset(one[:], 1.0)
-        unused = psum.tile([P, T], F32, name="back", bufs=4)
-
         def keep_warm(passes):
+            unused = psum.tile([P, T], F32, name="back", bufs=4)
             for repeat in range(passes):
                 nc.tensor.matmul(
                     out=unused[:],
@@ -338,6 +337,7 @@ def tile_l1regressionmoeactionhead_pa_t_kernel(
         for h in range(2):
             transpose_x(2, h)
             copy_x(2, h)
+        keep_warm(2)
         transpose_back(0, 1)
         multiply(0, 1)
         add_and_store(0, nc.gpsimd)
@@ -365,6 +365,7 @@ def tile_l1regressionmoeactionhead_pa_t_kernel(
         project(last - 1, 0)
         add_bias(last - 1, 0)
         project(last - 1, 1, name="xt")
+        keep_warm(1)
         transpose_back(last - 1, 0)
         multiply(last - 1, 0)
         add_and_store(last - 1, nc.gpsimd, 0, 1)
@@ -374,6 +375,7 @@ def tile_l1regressionmoeactionhead_pa_t_kernel(
         add_bias(last, 1, 0, half)
         project(last, 0, name="xt")
         project(last, 1, half, SUB)
+        keep_warm(1)
         transpose_back(last, 1, 0, half)
         sum_and_store(last - 1, 1, 0, SUB)
         multiply_turned(last, 0, 0, SUB)

@@ -112,35 +112,52 @@ def tile_l1regressionmoeactionhead_pa_t_kernel(
         load_bias(0)
         load_bias(1)
 
-        pace = keep.tile([P, 2, HALF], F32)
+        turns = keep.tile([P, 2, SUB, HALF], F32)
+        whole = keep.tile([P, 2, SUB, HALF], F32)
         ratio = ROPE_BASE ** (-1.0 / HALF)
         first = ((1.0, ratio, ratio**2, ratio**3), (ratio, -1.0, ratio**3, -(ratio**2)))
         for s in range(2):
             for j in range(4):
                 nc.vector.tensor_scalar_mul(
-                    out=pace[:, s, j : j + 1], in0=one[:], scalar1=first[s][j] / TWO_PI
+                    out=turns[:, s, :, j : j + 1],
+                    in0=position[:].unsqueeze(2),
+                    scalar1=first[s][j] / TWO_PI,
                 )
-        for width in (4, 16):
-            for k in range(1, 4):
-                nc.vector.tensor_scalar_mul(
-                    out=pace[:, :, k * width : (k + 1) * width],
-                    in0=pace[:, :, 0:width],
-                    scalar1=ratio ** (k * width),
-                )
-
-        turns = keep.tile([P, 2, SUB, HALF], F32)
-        whole = keep.tile([P, 2, SUB, HALF], F32)
-        nc.vector.tensor_tensor(
-            out=turns[:],
-            in0=position[:].unsqueeze(1).unsqueeze(3).to_broadcast([P, 2, SUB, HALF]),
-            in1=pace[:].unsqueeze(2).to_broadcast([P, 2, SUB, HALF]),
-            op=ALU.mult,
+        for k in range(1, 4):
+            nc.vector.tensor_scalar_mul(
+                out=turns[:, :, :, 4 * k : 4 * k + 4],
+                in0=turns[:, :, :, 0:4],
+                scalar1=ratio ** (4 * k),
+            )
+        for k in range(1, 4):
+            nc.vector.tensor_scalar_mul(
+                out=turns[:, 1, :, 16 * k : 16 * k + 16],
+                in0=turns[:, 1, :, 0:16],
+                scalar1=ratio ** (16 * k),
+            )
+        for k in range(1, 4):
+            nc.vector.tensor_scalar(
+                out=turns[:, 0, :, 16 * k : 16 * k + 16],
+                in0=turns[:, 0, :, 0:16],
+                scalar1=ratio ** (16 * k),
+                scalar2=0.25,
+                op0=ALU.mult,
+                op1=ALU.add,
+            )
+        nc.vector.tensor_scalar_add(
+            out=turns[:, 0, :, 0:16], in0=turns[:, 0, :, 0:16], scalar1=0.25
         )
-        nc.vector.tensor_scalar_add(out=turns[:, 0], in0=turns[:, 0], scalar1=0.25)
-        nc.vector.tensor_scalar(
-            out=whole[:], in0=turns[:], scalar1=ROUND, scalar2=ROUND, op0=ALU.add, op1=ALU.subtract
-        )
-        nc.vector.tensor_sub(out=turns[:], in0=turns[:], in1=whole[:])
+        for s in (1, 0):
+            nc.vector.tensor_scalar(
+                out=whole[:, s],
+                in0=turns[:, s],
+                scalar1=ROUND,
+                scalar2=ROUND,
+                op0=ALU.add,
+                op1=ALU.subtract,
+            )
+        for s in (1, 0):
+            nc.vector.tensor_sub(out=turns[:, s], in0=turns[:, s], in1=whole[:, s])
 
         table = keep.tile([P, SUB, 2, HALF], F32)
 
@@ -337,7 +354,6 @@ def tile_l1regressionmoeactionhead_pa_t_kernel(
         for h in range(2):
             transpose_x(2, h)
             copy_x(2, h)
-        keep_warm(2)
         transpose_back(0, 1)
         multiply(0, 1)
         add_and_store(0, nc.gpsimd)

@@ -339,7 +339,7 @@ def tile_l1regressionmoeactionhead_pa_t_kernel(
         transpose_x(1, 1)
         copy_x(1, 0, nc.vector.tensor_copy)
         add_bias(0, 0, 0, half)
-        copy_x(1, 1)
+        copy_x(1, 1, nc.vector.tensor_copy)
         project(0, 0, half, SUB)
         keep_warm(1)
         add_bias(0, 0, half, SUB)

import math
from contextlib import ExitStack

import concourse.masks as masks
import concourse.mybir as mybir

F32 = mybir.dt.float32
BF16 = mybir.dt.bfloat16
I32 = mybir.dt.int32
U32 = mybir.dt.uint32
U8 = mybir.dt.uint8
FP8X4 = mybir.dt.float8_e4m3fn_x4
FP4X4 = mybir.dt.float4_e2m1fn_x4
ALU = mybir.AluOpType
ACT = mybir.ActivationFunctionType

P = 128
BATCH = 16
T = 512
K = 512
D = 128
SUB = T // P
HALF = D // 2
ROPE_BASE = 10000.0
TWO_PI = 2.0 * math.pi
ROUND = 1.5 * 2.0**23

WARM_UP = 4

FLOPS = 2 * BATCH * T * K * 2 * D


def tile_l1regressionmoeactionhead_pa_t_kernel(
    tc, x, W_qa_words, W_qa_scales, b_qa, W_qt_words, W_qt_scales, b_qt, out_0, out_1
):
    nc = tc.nc
    outs = (out_0, out_1)
    weights = ((W_qa_words, W_qa_scales, b_qa), (W_qt_words, W_qt_scales, b_qt))

    with ExitStack() as ctx:
        keep = ctx.enter_context(tc.tile_pool(name="keep", bufs=1))
        work = ctx.enter_context(tc.tile_pool(name="work", bufs=2))
        psum = ctx.enter_context(tc.psum_pool(name="psum", bufs=2))
        ctx.enter_context(tc.manual_schedule())

        x_sb = keep.tile([P, BATCH, SUB, K], BF16)

        def load_x(n, queue, c0=0, c1=SUB):
            queue.dma_start(
                out=x_sb[:, n, c0:c1], in_=x[n].rearrange("(p c) k -> p c k", c=SUB)[:, c0:c1]
            )

        w_words = keep.tile([P, 2, 2 * D], U8, align_bytes=64)
        w_scales = keep.tile([P, 2, D], U8, align_bytes=64)
        nc.vector.memset(w_scales[:].bitcast(I32), 0)

        idle = keep.tile([P, P], BF16)
        nc.vector.memset(idle[:], 0.0)
        one = keep.tile([P, 1], F32)
        nc.vector.memset(one[:], 1.0)
        def keep_warm(passes):
            unused = psum.tile([P, T], F32, name="back", bufs=4)
            for repeat in range(passes):
                nc.tensor.matmul(
                    out=unused[:],
                    lhsT=idle[:],
                    rhs=idle[:, 0:1].to_broadcast([P, T]),
                    start=True,
                    stop=True,
                )

        keep_warm(WARM_UP)

        def load_weight(w):
            words, scales, bias = weights[w]
            nc.sync.dma_start(out=w_words[:, w, :].bitcast(I32), in_=words[0].bitcast(I32))
            for q in range(4):
                nc.sync.dma_start(
                    out=w_scales[32 * q : 32 * q + 4, w, :].bitcast(I32),
                    in_=scales[0, 4 * q : 4 * q + 4, :].bitcast(I32),
                )

        bias_of = []

        def load_bias(w):
            bias_column = keep.tile([P, 1], BF16, name="bias_column_%d" % w)
            nc.gpsimd.dma_start(out=bias_column[:], in_=weights[w][2].rearrange("(p o) -> p o", o=1))
            bias_of.append(bias_column)

        load_x(0, nc.scalar, 0, SUB // 2)
        load_x(0, nc.scalar, SUB // 2, SUB)
        load_weight(0)
        load_x(1, nc.scalar)
        load_x(2, nc.sync)
        load_weight(1)
        for n in range(3, BATCH):
            load_x(n, nc.sync)

        warm = keep.tile([P, 1], F32)
        nc.scalar.activation(out=warm[:], in_=one[:], func=ACT.Sin)

        position = keep.tile([P, SUB], F32)
        nc.gpsimd.iota(
            position[:],
            pattern=[[1, SUB]],
            base=0,
            channel_multiplier=SUB,
            allow_small_or_imprecise_dtypes=True,
        )
        ident = keep.tile([P, P], F32)
        masks.make_identity(nc, ident[:])
        load_bias(0)
        load_bias(1)

        turns = keep.tile([P, 2, SUB, HALF], F32)
        whole = keep.tile([P, 2, SUB, HALF], F32)
        ratio = ROPE_BASE ** (-1.0 / HALF)
        first = ((1.0, ratio, ratio**2, ratio**3), (ratio, -1.0, ratio**3, -(ratio**2)))
        for s in range(2):
            for j in range(4):
                nc.vector.tensor_scalar_mul(
                    out=turns[:, s, :, j : j + 1],
                    in0=position[:].unsqueeze(2),
                    scalar1=first[s][j] / TWO_PI,
                )
        for k in range(1, 4):
            nc.vector.tensor_scalar_mul(
                out=turns[:, :, :, 4 * k : 4 * k + 4],
                in0=turns[:, :, :, 0:4],
                scalar1=ratio ** (4 * k),
            )
        for k in range(1, 4):
            nc.vector.tensor_scalar_mul(
                out=turns[:, 1, :, 16 * k : 16 * k + 16],
                in0=turns[:, 1, :, 0:16],
                scalar1=ratio ** (16 * k),
            )
        for k in range(1, 4):
            nc.vector.tensor_scalar(
                out=turns[:, 0, :, 16 * k : 16 * k + 16],
                in0=turns[:, 0, :, 0:16],
                scalar1=ratio ** (16 * k),
                scalar2=0.25,
                op0=ALU.mult,
                op1=ALU.add,
            )
        nc.vector.tensor_scalar_add(
            out=turns[:, 0, :, 0:16], in0=turns[:, 0, :, 0:16], scalar1=0.25
        )
        for s in (1, 0):
            nc.vector.tensor_scalar(
                out=whole[:, s],
                in0=turns[:, s],
                scalar1=ROUND,
                scalar2=ROUND,
                op0=ALU.add,
                op1=ALU.subtract,
            )
        for s in (1, 0):
            nc.vector.tensor_sub(out=turns[:, s], in0=turns[:, s], in1=whole[:, s])

        table = keep.tile([P, SUB, 2, HALF], F32)

        def fill_tables():
            nc.scalar.activation(
                out=table[:].rearrange("p c s j -> p s c j"),
                in_=turns[:],
                func=ACT.Sin,
                scale=TWO_PI,
            )

        wide_table = keep.tile([P, SUB, 2, D], F32)
        turned_table = keep.tile([P, 2, SUB, P], F32)
        swap = keep.tile([P, P], F32)

        def widen_table(c0, c1):
            nc.scalar.copy(
                out=wide_table[:, c0:c1].rearrange("p c s (h j) -> p c s h j", h=2),
                in_=table[:, c0:c1].unsqueeze(3).to_broadcast([P, c1 - c0, 2, 2, HALF]),
            )

        def turn_table(s):
            bank = psum.tile([P, SUB, P], F32, name="back", bufs=4)
            for c in range(SUB):
                nc.tensor.transpose(bank[:, c, :], wide_table[:, c, s, :], ident[:])
            nc.scalar.copy(out=turned_table[:, s], in_=bank[:])

        def make_swap():
            nc.scalar.copy(
                out=swap[:].rearrange("p (i e) -> p i e", e=2),
                in_=ident[:].rearrange("p (i e) -> p i e", e=2)[:, :, ::-1],
            )

        xt_of = {}
        grouped_of = {}
        codes_of = {}
        acc_of = {}
        biased_of = {}
        back_of = {}

        def transpose_x(n, h):
            xt = psum.tile([P, 2, 2, P], F32, name="xt")
            for c in range(2):
                x_words = x_sb[:, n, 2 * h + c, :].bitcast(F32)
                for u in range(2):
                    nc.tensor.transpose(xt[:, c, u, :], x_words[:, u : K // 2 : 2], ident[:])
            xt_of[n, h] = xt

        def copy_x(n, h, copy=nc.scalar.copy):
            if n not in grouped_of:
                grouped_of[n] = work.tile([P, T * 4], BF16, align_bytes=64, name="grouped")
            words = grouped_of[n][:].bitcast(F32).rearrange("p (c t u) -> p c t u", c=SUB, u=2)
            copy(
                out=words[:, 2 * h : 2 * h + 2],
                in_=xt_of[n, h][:].rearrange("p c u t -> p c t u"),
            )

        def quantise(n, c0=0, c1=SUB):
            if n not in codes_of:
                codes = work.tile([P, T], U32, align_bytes=64, name="codes")
                plane = work.tile([P, T], U8, align_bytes=64, name="plane")
                codes_of[n] = (codes, plane)
            codes, plane = codes_of[n]
            nc.vector.quantize_mx(
                out=codes[:, c0 * P : c1 * P].bitcast(FP8X4),
                scales=plane[:, c0 * P : c1 * P],
                in_=grouped_of[n][:, c0 * P * 4 : c1 * P * 4],
            )

        def project(n, w, c0=0, c1=SUB, name="acc"):
            codes, plane = codes_of[n]
            acc = psum.tile([P, T], F32, name=name)
            nc.tensor.matmul_mx(
                out=acc[:, c0 * P : c1 * P],
                lhsT=w_words[:, w, :].bitcast(FP4X4),
                lhsT_scale=w_scales[:, w, :],
                rhs=codes[:, c0 * P : c1 * P].bitcast(FP8X4),
                rhs_scale=plane[:, c0 * P : c1 * P],
                start=True,
                stop=True,
            )
            acc_of[n, w, c0] = acc

        def add_bias(n, w, c0=0, c1=SUB):
            if (n, w) not in biased_of:
                biased_of[n, w] = work.tile([P, T], F32, name="biased", bufs=4)
            nc.scalar.activation(
                out=biased_of[n, w][:, c0 * P : c1 * P],
                in_=acc_of[n, w, c0][:, c0 * P : c1 * P],
                func=ACT.Identity,
                bias=bias_of[w][:],
            )

        def transpose_back(n, w, c0=0, c1=SUB):
            back = psum.tile([P, SUB, D], F32, name="back", bufs=4)
            for c in range(c0, c1):
                nc.tensor.transpose(
                    back[:, c, :], biased_of[n, w][:, c * P : (c + 1) * P], ident[:]
                )
            back_of[n, w, c0] = back

        products_of = {}
        result_of = {}
        turned_of = {}

        def multiply(n, w, c0=0, c1=SUB):
            if n not in products_of:
                products_of[n] = work.tile([P, 2, SUB, 2, D], F32, name="products", bufs=3)
            if n not in result_of:
                result_of[n] = work.tile([P, 2, SUB, D], F32, name="result", bufs=8)
            nc.vector.tensor_tensor(
                out=products_of[n][:, w, c0:c1].rearrange("p c s (h j) -> p c s h j", h=2),
                in0=back_of[n, w, c0][:, c0:c1]
                .rearrange("p c (h j) -> p c h j", h=2)
                .unsqueeze(2)
                .to_broadcast([P, c1 - c0, 2, 2, HALF]),
                in1=table[:, c0:c1].unsqueeze(3).to_broadcast([P, c1 - c0, 2, 2, HALF]),
                op=ALU.mult,
            )

        def add_and_store(n, adder, w0=0, w1=2, c0=0, c1=SUB):
            adder.tensor_tensor(
                out=result_of[n][:, w0:w1, c0:c1].rearrange("p w c (i e) -> p w c i e", e=2),
                in0=products_of[n][:, w0:w1, c0:c1, 0].rearrange("p w c (i e) -> p w c i e", e=2),
                in1=products_of[n][:, w0:w1, c0:c1, 1].rearrange("p w c (i e) -> p w c i e", e=2)[
                    :, :, :, :, ::-1
                ],
                op=ALU.add,
            )
            for w in range(w0, w1):
                nc.sync.dma_start(
                    out=outs[w][n, 0].rearrange("(p c) d -> p c d", c=SUB)[:, c0:c1],
                    in_=result_of[n][:, w, c0:c1],
                )

        def multiply_turned(n, w, c0, c1):
            turned = work.tile([P, 2, SUB, P], F32, name="turned")
            for s in range(2):
                nc.vector.scalar_tensor_tensor(
                    out=turned[:, s, c0:c1],
                    in0=acc_of[n, w, c0][:, c0 * P : c1 * P].rearrange("p (c t) -> p c t", t=P),
                    scalar=bias_of[w][:],
                    in1=turned_table[:, s, c0:c1],
                    op0=ALU.add,
                    op1=ALU.mult,
                )
            turned_of[n, w, c0] = turned

        def sum_and_store(n, w, c0, c1):
            turned = turned_of[n, w, c0]
            bank = psum.tile([P, SUB, D], F32, name="back", bufs=4)
            for c in range(c0, c1):
                for s, columns in ((0, ident), (1, swap)):
                    nc.tensor.matmul(
                        out=bank[:, c, :],
                        lhsT=turned[:, s, c, :],
                        rhs=columns[:],
                        is_transpose=True,
                        start=(s == 0),
                        stop=(s == 1),
                    )
            nc.scalar.copy(out=result_of[n][:, w, c0:c1], in_=bank[:, c0:c1])
            nc.sync.dma_start(
                out=outs[w][n, 0].rearrange("(p c) d -> p c d", c=SUB)[:, c0:c1],
                in_=result_of[n][:, w, c0:c1],
            )

        half = SUB // 2
        transpose_x(0, 0)
        transpose_x(0, 1)
        keep_warm(2)
        copy_x(0, 0)
        copy_x(0, 1)
        fill_tables()
        quantise(0, 0, half)
        quantise(0, half, SUB)
        transpose_x(1, 0)
        project(0, 0, 0, half)
        transpose_x(1, 1)
        copy_x(1, 0, nc.vector.tensor_copy)
        add_bias(0, 0, 0, half)
        copy_x(1, 1, nc.vector.tensor_copy)
        project(0, 0, half, SUB)
        keep_warm(1)
        add_bias(0, 0, half, SUB)
        transpose_back(0, 0, 0, half)
        multiply(0, 0, 0, half)
        quantise(1)
        project(0, 1)
        keep_warm(1)
        add_bias(0, 1)
        transpose_back(0, 0, half, SUB)
        multiply(0, 0, half, SUB)
        for h in range(2):
            transpose_x(2, h)
            copy_x(2, h)
        transpose_back(0, 1)
        multiply(0, 1)
        add_and_store(0, nc.gpsimd)
        quantise(2)
        for n in range(1, BATCH - 2):
            for w in range(2):
                project(n, w)
                add_bias(n, w)
            for h in range(2):
                transpose_x(n + 2, h)
                copy_x(n + 2, h)
            for w in range(2):
                transpose_back(n, w)
                multiply(n, w)
            add_and_store(n, nc.gpsimd)
            quantise(n + 2)
            if n == 4:
                make_swap()
                widen_table(0, half)
            if n == 5:
                widen_table(half, SUB)
            if n in (6, 7):
                turn_table(n - 6)
        last = BATCH - 1
        project(last - 1, 0)
        add_bias(last - 1, 0)
        project(last - 1, 1, name="xt")
        keep_warm(1)
        transpose_back(last - 1, 0)
        multiply(last - 1, 0)
        add_and_store(last - 1, nc.gpsimd, 0, 1)
        multiply_turned(last - 1, 1, 0, SUB)
        result_of[last] = work.tile([P, 2, SUB, D], F32, name="result", bufs=8)
        project(last, 1, 0, half)
        add_bias(last, 1, 0, half)
        project(last, 0, name="xt")
        project(last, 1, half, SUB)
        keep_warm(1)
        transpose_back(last, 1, 0, half)
        sum_and_store(last - 1, 1, 0, SUB)
        multiply_turned(last, 0, 0, SUB)
        sum_and_store(last, 0, 0, SUB)
        multiply_turned(last, 1, half, SUB)
        sum_and_store(last, 1, half, SUB)
        multiply(last, 1, 0, half)
        add_and_store(last, nc.vector, 1, 2, 0, half)
